import numpy as np
import ml_dtypes


def mxq(x, axis, fmt="e4m3"):
    dtype, down = {"e4m3": (ml_dtypes.float8_e4m3fn, 7), "e5m2": (ml_dtypes.float8_e5m2, 14)}[fmt]
    v = np.moveaxis(np.asarray(x, np.float32).astype(ml_dtypes.bfloat16).astype(np.float64), axis, -1)
    blocks = v.reshape(v.shape[:-1] + (-1, 32))
    amax = np.abs(blocks).max(-1, keepdims=True)
    byte = np.maximum(np.where(amax > 0, np.frexp(amax)[1] - 1 + 127, 0) - down, 1)
    scale = np.exp2(byte - 127.0)
    codes = (blocks / scale).astype(np.float32).astype(dtype).astype(np.float64)
    return np.moveaxis((codes * scale).reshape(v.shape), -1, axis)


WIDE = False


def mx_kscale(k):
    if not WIDE:
        return np.ones(k)
    levels = np.array([10, -10, 5, -5, 0])
    if k % 512:
        return np.exp2(np.random.permutation(np.resize(levels, k // 32))).repeat(32)
    a = np.empty((k // 512, 16))
    for p in range(k // 512):
        a[p, :8] = np.random.permutation(np.resize(levels, 8))
        for g in range(8):
            far = levels[np.abs(levels - a[p, g]) >= 10]
            a[p, g + 8] = far[np.random.randint(len(far))]
    return np.exp2(a.ravel()).repeat(32)


BF16 = ml_dtypes.bfloat16


def bf(x):
    return np.asarray(x, np.float32).astype(BF16)


def f64(x):
    return np.asarray(x).astype(np.float64)


B, S, K, N = 4, 128, 2048, 5632


def setup_inputs():
    s = mx_kscale(K)
    return {"x": bf(np.random.standard_normal((B, S, K)) * s),
            "weight": bf(np.random.standard_normal((N, K)) * (1.0 / np.sqrt(K)) / s[None, :]),
            "wscales": bf(np.random.uniform(0.5, 1.5, (N, 1))),
            "bias": bf(np.random.standard_normal((1, N)) * 0.3)}


def reference(x, weight, wscales, bias):
    x2 = f64(x).reshape(-1, weight.shape[1])
    w_dequant = f64(weight) * f64(wscales)
    out = mxq(x2, 1, "e4m3") @ mxq(w_dequant, 1, "e4m3").T
    out = out.reshape(*x.shape[:-1], weight.shape[0])
    out = out + f64(bias)
    return out

@@ -1,0 +1,263 @@
+from contextlib import ExitStack
+
+import concourse.mybir as mybir
+from concourse.masks import make_identity
+
+FP8X4 = mybir.dt.float8_e4m3fn_x4
+BF16 = mybir.dt.bfloat16
+F32 = mybir.dt.float32
+U32 = mybir.dt.uint32
+U8 = mybir.dt.uint8
+I32 = mybir.dt.int32
+MULT = mybir.AluOpType.mult
+ADD = mybir.AluOpType.add
+
+P = 128
+TOKENS = 512
+K = 2048
+N = 5632
+FLOPS = 2 * TOKENS * K * N
+
+PASSES = K // 512
+MT = TOKENS // P
+UNIT = 256
+UNITS = N // UNIT
+PIECE = 1024
+PIECES = (N + PIECE - 1) // PIECE
+BIAS_ROW = 32
+RAW_BUFS = 7
+RUN = 16
+GROUP_SIZES = (4, 4, 4, 4, 2, 2, 1, 1)
+
+
+def tile_unicorelinearfp4_kernel(tc, x, weight, wscales, bias, out):
+    nc = tc.nc
+    x_rows = x.flatten_outer_dims().rearrange("(p m) k -> p m k", m=MT)
+    out_rows = out.flatten_outer_dims().rearrange("(p m) n -> p m n", m=MT)
+    ws_vec = wscales.rearrange("n o -> (n o)")
+    bias_vec = bias.rearrange("o n -> (o n)")
+
+    group_of = {}
+    group_start = []
+    first = 0
+    for gi, size in enumerate(GROUP_SIZES):
+        group_start.append(first)
+        for u in range(first, first + size):
+            group_of[u] = gi
+        first += size
+    assert first == UNITS
+
+    with ExitStack() as ctx:
+        const = ctx.enter_context(tc.tile_pool(name="const", bufs=1))
+        xg_pool = ctx.enter_context(tc.tile_pool(name="xg", bufs=2))
+        raw_pool = ctx.enter_context(tc.tile_pool(name="raw", bufs=RAW_BUFS))
+        scl_pool = ctx.enter_context(tc.tile_pool(name="scl", bufs=3))
+        grp_pool = ctx.enter_context(tc.tile_pool(name="grp", bufs=3))
+        code_pool = ctx.enter_context(tc.tile_pool(name="code", bufs=4))
+        stage_pool = ctx.enter_context(tc.tile_pool(name="stage", bufs=3))
+        tp_pool = ctx.enter_context(tc.psum_pool(name="tp", bufs=4))
+        acc_pool = ctx.enter_context(tc.psum_pool(name="acc", bufs=4))
+        ctx.enter_context(tc.manual_schedule())
+
+        ident = const.tile([P, P], F32, name="ident")
+        vrows = const.tile([P, UNIT], BF16, name="vrows")
+        pv = const.tile([P, P], F32, name="pv")
+        bias_sb = const.tile([P, N], BF16, name="bias_sb")
+        xraw = const.tile([P, MT, K], BF16, name="xraw")
+        xperm = const.tile([P, MT, K], BF16, name="xperm")
+        xcodes = const.tile([P, MT, PASSES * P], U32, name="xcodes", align_bytes=64)
+        xplane = const.tile([P, MT, PASSES * P], U8, name="xplane", align_bytes=64)
+        ws_pp = pv[:, 0:UNITS].bitcast(BF16)
+
+        raw = {}
+        scl = {}
+        tp = {}
+        grp = {}
+        codes = {}
+        plane = {}
+        acc = {}
+        stage = {}
+
+        def spread_bias(q, on_vector):
+            units = min(4, UNITS - 4 * q)
+            bank = acc_pool.tile([P, 512], F32, name="sp%d" % q, tag="acc")
+            for u in range(units):
+                r = BIAS_ROW + 4 * q + u
+                nc.tensor.transpose(
+                    bank[:, u * P : (u + 1) * P], pv[:, r : r + 1].to_broadcast([P, P]), ident[:]
+                )
+            words = bias_sb[:, q * PIECE : q * PIECE + units * UNIT].bitcast(F32)
+            if on_vector:
+                nc.vector.tensor_copy(out=words, in_=bank[:, 0 : units * P])
+            else:
+                nc.scalar.copy(out=words, in_=bank[:, 0 : units * P])
+
+        def load_unit(i):
+            raw[i] = raw_pool.tile([P, 2, K], BF16, name="raw%d" % i, tag="raw")
+            rows = weight[i * UNIT : (i + 1) * UNIT, :].rearrange("(p j) k -> p j k", j=2)
+            nc.sync.dma_start(out=raw[i][:], in_=rows)
+
+        def prescale_unit(i):
+            scl[i] = scl_pool.tile([P, 2, K], BF16, name="scl%d" % i, tag="scl")
+            for j in range(2):
+                nc.vector.tensor_scalar(
+                    out=scl[i][:, j, :].rearrange("p (u b i) -> p u b i", u=2, i=RUN),
+                    in0=raw[i][:, j, :].rearrange("p (b u i) -> p u b i", u=2, i=RUN),
+                    scalar1=ws_pp[:, 2 * i + j : 2 * i + j + 1],
+                    scalar2=None,
+                    op0=MULT,
+                )
+
+        def transpose_unit(i):
+            grp[i] = grp_pool.tile([P, PASSES * 4 * UNIT], BF16, name="grp%d" % i, tag="grp", align_bytes=64)
+            for g in range(PASSES):
+                bank = tp_pool.tile([P, 512], F32, name="tp%d_%d" % (i, g), tag="tp")
+                for j in range(2):
+                    words = scl[i][:, j, :].bitcast(F32)
+                    for h in range(2):
+                        s = 2 * j + h
+                        blk = PASSES * h + g
+                        nc.tensor.transpose(
+                            bank[:, s * P : (s + 1) * P],
+                            words[:, blk * P : (blk + 1) * P],
+                            ident[:],
+                        )
+                nc.scalar.copy(
+                    out=grp[i][:, g * 1024 : (g + 1) * 1024].bitcast(F32).rearrange("p (c s) -> p c s", s=4),
+                    in_=bank[:].rearrange("p (s c) -> p c s", s=4),
+                )
+
+        def quantise_unit(i):
+            codes[i] = code_pool.tile([P, PASSES * UNIT], U32, name="codes%d" % i, tag="codes", align_bytes=64)
+            plane[i] = code_pool.tile([P, PASSES * UNIT], U8, name="plane%d" % i, tag="plane", align_bytes=64)
+            nc.vector.quantize_mx(out=codes[i][:].bitcast(FP8X4), scales=plane[i][:], in_=grp[i][:])
+
+        def multiply_unit(i, b):
+            bank = acc_pool.tile([P, 512], F32, name="acc%d_%d" % (i, b), tag="acc")
+            acc[(i, b)] = bank
+            for mm in range(2):
+                m = 2 * b + mm
+                for g in range(PASSES):
+                    nc.tensor.matmul_mx(
+                        out=bank[:, mm * UNIT : (mm + 1) * UNIT],
+                        lhsT=xcodes[:, m, g * P : (g + 1) * P].bitcast(FP8X4),
+                        lhsT_scale=xplane[:, m, g * P : (g + 1) * P],
+                        rhs=codes[i][:, g * UNIT : (g + 1) * UNIT].bitcast(FP8X4),
+                        rhs_scale=plane[i][:, g * UNIT : (g + 1) * UNIT],
+                        start=(g == 0),
+                        stop=(g == PASSES - 1),
+                    )
+
+        def finish_unit(i):
+            gi = group_of[i]
+            if i == group_start[gi]:
+                stage[gi] = stage_pool.tile([P, MT, 4 * UNIT], F32, name="stage%d" % gi, tag="stage")
+            off = (i - group_start[gi]) * UNIT
+            row = bias_sb[:, i * UNIT : (i + 1) * UNIT].unsqueeze(1).to_broadcast([P, 2, UNIT])
+            for b in range(2):
+                nc.vector.tensor_tensor(
+                    out=stage[gi][:, 2 * b : 2 * b + 2, off : off + UNIT],
+                    in0=acc[(i, b)][:].rearrange("p (m n) -> p m n", m=2),
+                    in1=row,
+                    op=ADD,
+                )
+                if i == UNITS - 1:
+                    nc.sync.dma_start(
+                        out=out_rows[:, 2 * b : 2 * b + 2, i * UNIT : (i + 1) * UNIT],
+                        in_=stage[gi][:, 2 * b : 2 * b + 2, off : off + UNIT],
+                    )
+            if i == group_start[gi] + GROUP_SIZES[gi] - 1 and i < UNITS - 1:
+                a = group_start[gi] * UNIT
+                w = GROUP_SIZES[gi] * UNIT
+                nc.sync.dma_start(out=out_rows[:, :, a : a + w], in_=stage[gi][:, :, 0:w])
+
+        xg = {}
+
+        def transpose_x(m, second_on_vector):
+            xg[m] = xg_pool.tile([P, PASSES * 4 * P], BF16, name="xg%d" % m, tag="xg", align_bytes=64)
+            nc.vector.tensor_copy(
+                out=xperm[:, m, :].rearrange("p (u b i) -> p u b i", u=2, i=RUN),
+                in_=xraw[:, m, :].rearrange("p (b u i) -> p u b i", u=2, i=RUN),
+            )
+            words = xperm[:, m, :].bitcast(F32)
+            for b in range(2):
+                bank = tp_pool.tile([P, 512], F32, name="tpx%d_%d" % (m, b), tag="tp")
+                for s in range(4):
+                    blk = PASSES * (s % 2) + 2 * b + s // 2
+                    nc.tensor.transpose(
+                        bank[:, s * P : (s + 1) * P], words[:, blk * P : (blk + 1) * P], ident[:]
+                    )
+                dst = xg[m][:, b * 1024 : (b + 1) * 1024].bitcast(F32).rearrange("p (g c h) -> p g c h", g=2, h=2)
+                src = bank[:].rearrange("p (g h c) -> p g c h", g=2, h=2)
+                if b == 1 and second_on_vector:
+                    nc.vector.tensor_copy(out=dst, in_=src)
+                else:
+                    nc.scalar.copy(out=dst, in_=src)
+
+        def quantise_x(m):
+            nc.vector.quantize_mx(out=xcodes[:, m, :].bitcast(FP8X4), scales=xplane[:, m, :], in_=xg[m][:])
+
+        make_identity(nc, ident[:])
+        nc.vector.memset(vrows[:].bitcast(I32), 0)
+        nc.sync.dma_start(out=vrows[0:UNITS, :], in_=ws_vec.rearrange("(r n) -> r n", n=UNIT))
+        nc.sync.dma_start(
+            out=vrows[BIAS_ROW : BIAS_ROW + UNITS, :], in_=bias_vec.rearrange("(r n) -> r n", n=UNIT)
+        )
+        load_unit(0)
+        for m in range(MT):
+            nc.sync.dma_start(out=xraw[:, m, :], in_=x_rows[:, m, :])
+        for i in range(1, RAW_BUFS):
+            load_unit(i)
+
+        pv_bank = acc_pool.tile([P, 512], F32, name="pv_bank", tag="acc")
+        nc.tensor.transpose(pv_bank[:, 0:P], vrows[:].bitcast(F32), ident[:])
+        nc.vector.tensor_copy(out=pv[:], in_=pv_bank[:, 0:P])
+        for q in range(PIECES):
+            spread_bias(q, q == 1)
+
+        state = {"ps": 0, "t": 0, "q": 0, "load": RAW_BUFS}
+
+        def next_prescale():
+            prescale_unit(state["ps"])
+            if state["load"] < UNITS:
+                load_unit(state["load"])
+                state["load"] += 1
+            state["ps"] += 1
+
+        def next_transpose():
+            while state["ps"] <= state["t"]:
+                next_prescale()
+            transpose_unit(state["t"])
+            state["t"] += 1
+
+        def next_quantise():
+            quantise_unit(state["q"])
+            state["q"] += 1
+
+        next_transpose()
+        transpose_x(0, True)
+        next_quantise()
+        transpose_x(1, True)
+        quantise_x(0)
+        quantise_x(1)
+        next_prescale()
+        transpose_x(2, False)
+        quantise_x(2)
+        transpose_x(3, False)
+        quantise_x(3)
+        next_prescale()
+        multiply_unit(0, 0)
+        for k in range(UNITS + 1):
+            lead = 2 if k == 0 else k + 3
+            while state["t"] < min(UNITS, lead):
+                next_transpose()
+            while state["ps"] < min(UNITS, state["t"] + 1):
+                next_prescale()
+            if k >= 1:
+                finish_unit(k - 1)
+            while state["q"] < min(UNITS, state["t"], k + 3):
+                next_quantise()
+            if k < UNITS:
+                if k > 0:
+                    multiply_unit(k, 0)
+                multiply_unit(k, 1)

@@ -26,7 +26,6 @@ PIECE = 1024
 PIECES = (N + PIECE - 1) // PIECE
 BIAS_ROW = 32
 RAW_BUFS = 7
-RUN = 16
 GROUP_SIZES = (4, 4, 4, 4, 2, 2, 1, 1)
 
 
@@ -64,7 +63,6 @@ def tile_unicorelinearfp4_kernel(tc, x, weight, wscales, bias, out):
         pv = const.tile([P, P], F32, name="pv")
         bias_sb = const.tile([P, N], BF16, name="bias_sb")
         xraw = const.tile([P, MT, K], BF16, name="xraw")
-        xperm = const.tile([P, MT, K], BF16, name="xperm")
         xcodes = const.tile([P, MT, PASSES * P], U32, name="xcodes", align_bytes=64)
         xplane = const.tile([P, MT, PASSES * P], U8, name="xplane", align_bytes=64)
         ws_pp = pv[:, 0:UNITS].bitcast(BF16)
@@ -101,8 +99,8 @@ def tile_unicorelinearfp4_kernel(tc, x, weight, wscales, bias, out):
             scl[i] = scl_pool.tile([P, 2, K], BF16, name="scl%d" % i, tag="scl")
             for j in range(2):
                 nc.vector.tensor_scalar(
-                    out=scl[i][:, j, :].rearrange("p (u b i) -> p u b i", u=2, i=RUN),
-                    in0=raw[i][:, j, :].rearrange("p (b u i) -> p u b i", u=2, i=RUN),
+                    out=scl[i][:, j, :].rearrange("p (u w e) -> p u w e", u=2, e=2),
+                    in0=raw[i][:, j, :].rearrange("p (w u e) -> p u w e", u=2, e=2),
                     scalar1=ws_pp[:, 2 * i + j : 2 * i + j + 1],
                     scalar2=None,
                     op0=MULT,
@@ -175,17 +173,13 @@ def tile_unicorelinearfp4_kernel(tc, x, weight, wscales, bias, out):
 
         def transpose_x(m, second_on_vector):
             xg[m] = xg_pool.tile([P, PASSES * 4 * P], BF16, name="xg%d" % m, tag="xg", align_bytes=64)
-            nc.vector.tensor_copy(
-                out=xperm[:, m, :].rearrange("p (u b i) -> p u b i", u=2, i=RUN),
-                in_=xraw[:, m, :].rearrange("p (b u i) -> p u b i", u=2, i=RUN),
-            )
-            words = xperm[:, m, :].bitcast(F32)
+            words = xraw[:, m, :].bitcast(F32)
             for b in range(2):
                 bank = tp_pool.tile([P, 512], F32, name="tpx%d_%d" % (m, b), tag="tp")
                 for s in range(4):
-                    blk = PASSES * (s % 2) + 2 * b + s // 2
+                    first = 2 * P * (2 * b + s // 2)
                     nc.tensor.transpose(
-                        bank[:, s * P : (s + 1) * P], words[:, blk * P : (blk + 1) * P], ident[:]
+                        bank[:, s * P : (s + 1) * P], words[:, first + s % 2 : first + 2 * P : 2], ident[:]
                     )
                 dst = xg[m][:, b * 1024 : (b + 1) * 1024].bitcast(F32).rearrange("p (g c h) -> p g c h", g=2, h=2)
                 src = bank[:].rearrange("p (g h c) -> p g c h", g=2, h=2)

@@ -27,6 +27,7 @@ PIECES = (N + PIECE - 1) // PIECE
 BIAS_ROW = 32
 RAW_BUFS = 7
 GROUP_SIZES = (4, 4, 4, 4, 2, 2, 1, 1)
+HALF = K // 2
 
 
 def tile_unicorelinearfp4_kernel(tc, x, weight, wscales, bias, out):
@@ -48,6 +49,7 @@ def tile_unicorelinearfp4_kernel(tc, x, weight, wscales, bias, out):
 
     with ExitStack() as ctx:
         const = ctx.enter_context(tc.tile_pool(name="const", bufs=1))
+        xdei_pool = ctx.enter_context(tc.tile_pool(name="xdei", bufs=2))
         xg_pool = ctx.enter_context(tc.tile_pool(name="xg", bufs=2))
         raw_pool = ctx.enter_context(tc.tile_pool(name="raw", bufs=RAW_BUFS))
         scl_pool = ctx.enter_context(tc.tile_pool(name="scl", bufs=3))
@@ -59,6 +61,7 @@ def tile_unicorelinearfp4_kernel(tc, x, weight, wscales, bias, out):
         ctx.enter_context(tc.manual_schedule())
 
         ident = const.tile([P, P], F32, name="ident")
+        zeros = const.tile([P, 512], BF16, name="zeros")
         vrows = const.tile([P, UNIT], BF16, name="vrows")
         pv = const.tile([P, P], F32, name="pv")
         bias_sb = const.tile([P, N], BF16, name="bias_sb")
@@ -69,12 +72,16 @@ def tile_unicorelinearfp4_kernel(tc, x, weight, wscales, bias, out):
 
         raw = {}
         scl = {}
-        tp = {}
         grp = {}
         codes = {}
         plane = {}
         acc = {}
         stage = {}
+        xg = {}
+
+        def warm_up(bank, n):
+            for r in range(n):
+                nc.tensor.matmul(bank[:], lhsT=zeros[:, 0:P], rhs=zeros[:], start=True, stop=True)
 
         def spread_bias(q, on_vector):
             units = min(4, UNITS - 4 * q)
@@ -90,100 +97,134 @@ def tile_unicorelinearfp4_kernel(tc, x, weight, wscales, bias, out):
             else:
                 nc.scalar.copy(out=words, in_=bank[:, 0 : units * P])
 
-        def load_unit(i):
-            raw[i] = raw_pool.tile([P, 2, K], BF16, name="raw%d" % i, tag="raw")
-            rows = weight[i * UNIT : (i + 1) * UNIT, :].rearrange("(p j) k -> p j k", j=2)
-            nc.sync.dma_start(out=raw[i][:], in_=rows)
+        def unit_rows(i):
+            return weight[i * UNIT : (i + 1) * UNIT, :].rearrange("(p j) k -> p j k", j=2)
 
-        def prescale_unit(i):
-            scl[i] = scl_pool.tile([P, 2, K], BF16, name="scl%d" % i, tag="scl")
+        def load_unit(i):
+            for a in range(parts(i)):
+                load_part(i, a)
+
+        def parts(i):
+            return 2 if i == 0 else 1
+
+        def load_part(i, a):
+            n = parts(i)
+            w = K // n
+            if i not in raw:
+                raw[i] = raw_pool.tile([P, n, 2, w], BF16, name="raw%d" % i, tag="raw")
+            nc.sync.dma_start(out=raw[i][:, a, :, :], in_=unit_rows(i)[:, :, a * w : (a + 1) * w])
+
+        def prescale(i, a):
+            n = parts(i)
+            if i not in scl:
+                scl[i] = scl_pool.tile([P, n, 2, K // n], BF16, name="scl%d" % i, tag="scl")
             for j in range(2):
                 nc.vector.tensor_scalar(
-                    out=scl[i][:, j, :].rearrange("p (u w e) -> p u w e", u=2, e=2),
-                    in0=raw[i][:, j, :].rearrange("p (w u e) -> p u w e", u=2, e=2),
+                    out=scl[i][:, a, j, :].rearrange("p (u w e) -> p u w e", u=2, e=2),
+                    in0=raw[i][:, a, j, :].rearrange("p (w u e) -> p u w e", u=2, e=2),
                     scalar1=ws_pp[:, 2 * i + j : 2 * i + j + 1],
                     scalar2=None,
                     op0=MULT,
                 )
 
+        def prescale_unit(i):
+            for a in range(parts(i)):
+                prescale(i, a)
+
+        def transpose_pass(i, g, dummies=0):
+            if i not in grp:
+                grp[i] = grp_pool.tile([P, PASSES * 4 * UNIT], BF16, name="grp%d" % i, tag="grp", align_bytes=64)
+            bank = tp_pool.tile([P, 512], F32, name="tp%d_%d" % (i, g), tag="tp")
+            warm_up(bank, dummies)
+            per = PASSES // parts(i)
+            for j in range(2):
+                words = scl[i][:, g // per, j, :].bitcast(F32)
+                for h in range(2):
+                    s = 2 * j + h
+                    blk = per * h + g % per
+                    nc.tensor.transpose(
+                        bank[:, s * P : (s + 1) * P], words[:, blk * P : (blk + 1) * P], ident[:]
+                    )
+            nc.scalar.copy(
+                out=grp[i][:, g * 1024 : (g + 1) * 1024].bitcast(F32).rearrange("p (c s) -> p c s", s=4),
+                in_=bank[:].rearrange("p (s c) -> p c s", s=4),
+            )
+
         def transpose_unit(i):
-            grp[i] = grp_pool.tile([P, PASSES * 4 * UNIT], BF16, name="grp%d" % i, tag="grp", align_bytes=64)
             for g in range(PASSES):
-                bank = tp_pool.tile([P, 512], F32, name="tp%d_%d" % (i, g), tag="tp")
-                for j in range(2):
-                    words = scl[i][:, j, :].bitcast(F32)
-                    for h in range(2):
-                        s = 2 * j + h
-                        blk = PASSES * h + g
-                        nc.tensor.transpose(
-                            bank[:, s * P : (s + 1) * P],
-                            words[:, blk * P : (blk + 1) * P],
-                            ident[:],
-                        )
-                nc.scalar.copy(
-                    out=grp[i][:, g * 1024 : (g + 1) * 1024].bitcast(F32).rearrange("p (c s) -> p c s", s=4),
-                    in_=bank[:].rearrange("p (s c) -> p c s", s=4),
+                transpose_pass(i, g)
+
+        def quantise(i, g0, g1):
+            if i not in codes:
+                codes[i] = code_pool.tile([P, PASSES * UNIT], U32, name="codes%d" % i, tag="codes", align_bytes=64)
+                plane[i] = code_pool.tile([P, PASSES * UNIT], U8, name="plane%d" % i, tag="plane", align_bytes=64)
+            cols = slice(g0 * UNIT, g1 * UNIT)
+            nc.vector.quantize_mx(
+                out=codes[i][:, cols].bitcast(FP8X4),
+                scales=plane[i][:, cols],
+                in_=grp[i][:, 4 * g0 * UNIT : 4 * g1 * UNIT],
+            )
+
+        def multiply(i, m):
+            b = m // 2
+            if (i, b) not in acc:
+                acc[(i, b)] = acc_pool.tile([P, 512], F32, name="acc%d_%d" % (i, b), tag="acc")
+            for g in range(PASSES):
+                nc.tensor.matmul_mx(
+                    out=acc[(i, b)][:, (m % 2) * UNIT : (m % 2 + 1) * UNIT],
+                    lhsT=xcodes[:, m, g * P : (g + 1) * P].bitcast(FP8X4),
+                    lhsT_scale=xplane[:, m, g * P : (g + 1) * P],
+                    rhs=codes[i][:, g * UNIT : (g + 1) * UNIT].bitcast(FP8X4),
+                    rhs_scale=plane[i][:, g * UNIT : (g + 1) * UNIT],
+                    start=(g == 0),
+                    stop=(g == PASSES - 1),
                 )
 
-        def quantise_unit(i):
-            codes[i] = code_pool.tile([P, PASSES * UNIT], U32, name="codes%d" % i, tag="codes", align_bytes=64)
-            plane[i] = code_pool.tile([P, PASSES * UNIT], U8, name="plane%d" % i, tag="plane", align_bytes=64)
-            nc.vector.quantize_mx(out=codes[i][:].bitcast(FP8X4), scales=plane[i][:], in_=grp[i][:])
-
-        def multiply_unit(i, b):
-            bank = acc_pool.tile([P, 512], F32, name="acc%d_%d" % (i, b), tag="acc")
-            acc[(i, b)] = bank
-            for mm in range(2):
-                m = 2 * b + mm
-                for g in range(PASSES):
-                    nc.tensor.matmul_mx(
-                        out=bank[:, mm * UNIT : (mm + 1) * UNIT],
-                        lhsT=xcodes[:, m, g * P : (g + 1) * P].bitcast(FP8X4),
-                        lhsT_scale=xplane[:, m, g * P : (g + 1) * P],
-                        rhs=codes[i][:, g * UNIT : (g + 1) * UNIT].bitcast(FP8X4),
-                        rhs_scale=plane[i][:, g * UNIT : (g + 1) * UNIT],
-                        start=(g == 0),
-                        stop=(g == PASSES - 1),
-                    )
-
-        def finish_unit(i):
+        def finish(i, b):
             gi = group_of[i]
-            if i == group_start[gi]:
+            if gi not in stage:
                 stage[gi] = stage_pool.tile([P, MT, 4 * UNIT], F32, name="stage%d" % gi, tag="stage")
             off = (i - group_start[gi]) * UNIT
             row = bias_sb[:, i * UNIT : (i + 1) * UNIT].unsqueeze(1).to_broadcast([P, 2, UNIT])
-            for b in range(2):
-                nc.vector.tensor_tensor(
-                    out=stage[gi][:, 2 * b : 2 * b + 2, off : off + UNIT],
-                    in0=acc[(i, b)][:].rearrange("p (m n) -> p m n", m=2),
-                    in1=row,
-                    op=ADD,
+            nc.vector.tensor_tensor(
+                out=stage[gi][:, 2 * b : 2 * b + 2, off : off + UNIT],
+                in0=acc[(i, b)][:].rearrange("p (m n) -> p m n", m=2),
+                in1=row,
+                op=ADD,
+            )
+            if i == UNITS - 1:
+                nc.sync.dma_start(
+                    out=out_rows[:, 2 * b : 2 * b + 2, i * UNIT : (i + 1) * UNIT],
+                    in_=stage[gi][:, 2 * b : 2 * b + 2, off : off + UNIT],
                 )
-                if i == UNITS - 1:
-                    nc.sync.dma_start(
-                        out=out_rows[:, 2 * b : 2 * b + 2, i * UNIT : (i + 1) * UNIT],
-                        in_=stage[gi][:, 2 * b : 2 * b + 2, off : off + UNIT],
-                    )
-            if i == group_start[gi] + GROUP_SIZES[gi] - 1 and i < UNITS - 1:
+            elif b == 1 and i == group_start[gi] + GROUP_SIZES[gi] - 1:
                 a = group_start[gi] * UNIT
                 w = GROUP_SIZES[gi] * UNIT
                 nc.sync.dma_start(out=out_rows[:, :, a : a + w], in_=stage[gi][:, :, 0:w])
 
-        xg = {}
+        xdei = {}
 
-        def transpose_x(m, second_on_vector):
+        def split_x(m):
+            xdei[m] = xdei_pool.tile([P, K], BF16, name="xdei%d" % m, tag="xdei")
+            nc.vector.tensor_copy(
+                out=xdei[m][:].rearrange("p (u w e) -> p u w e", u=2, e=2),
+                in_=xraw[:, m, :].rearrange("p (w u e) -> p u w e", u=2, e=2),
+            )
+
+        def transpose_x(m, engines="ss", dummies=0):
             xg[m] = xg_pool.tile([P, PASSES * 4 * P], BF16, name="xg%d" % m, tag="xg", align_bytes=64)
-            words = xraw[:, m, :].bitcast(F32)
+            words = xdei[m][:].bitcast(F32)
             for b in range(2):
                 bank = tp_pool.tile([P, 512], F32, name="tpx%d_%d" % (m, b), tag="tp")
+                warm_up(bank, dummies)
                 for s in range(4):
-                    first = 2 * P * (2 * b + s // 2)
+                    blk = PASSES * (s % 2) + 2 * b + s // 2
                     nc.tensor.transpose(
-                        bank[:, s * P : (s + 1) * P], words[:, first + s % 2 : first + 2 * P : 2], ident[:]
+                        bank[:, s * P : (s + 1) * P], words[:, blk * P : (blk + 1) * P], ident[:]
                     )
                 dst = xg[m][:, b * 1024 : (b + 1) * 1024].bitcast(F32).rearrange("p (g c h) -> p g c h", g=2, h=2)
                 src = bank[:].rearrange("p (g h c) -> p g c h", g=2, h=2)
-                if b == 1 and second_on_vector:
+                if engines[b] == "v":
                     nc.vector.tensor_copy(out=dst, in_=src)
                 else:
                     nc.scalar.copy(out=dst, in_=src)
@@ -191,67 +232,79 @@ def tile_unicorelinearfp4_kernel(tc, x, weight, wscales, bias, out):
         def quantise_x(m):
             nc.vector.quantize_mx(out=xcodes[:, m, :].bitcast(FP8X4), scales=xplane[:, m, :], in_=xg[m][:])
 
-        make_identity(nc, ident[:])
+        nc.vector.memset(zeros[:].bitcast(I32), 0)
         nc.vector.memset(vrows[:].bitcast(I32), 0)
-        nc.sync.dma_start(out=vrows[0:UNITS, :], in_=ws_vec.rearrange("(r n) -> r n", n=UNIT))
-        nc.sync.dma_start(
+        make_identity(nc, ident[:])
+        nc.scalar.dma_start(out=vrows[0:UNITS, :], in_=ws_vec.rearrange("(r n) -> r n", n=UNIT))
+        nc.scalar.dma_start(
             out=vrows[BIAS_ROW : BIAS_ROW + UNITS, :], in_=bias_vec.rearrange("(r n) -> r n", n=UNIT)
         )
+        nc.sync.dma_start(out=xraw[:, 0, :], in_=x_rows[:, 0, :])
         load_unit(0)
-        for m in range(MT):
+        for m in range(1, MT):
             nc.sync.dma_start(out=xraw[:, m, :], in_=x_rows[:, m, :])
         for i in range(1, RAW_BUFS):
             load_unit(i)
 
+        warm_bank = tp_pool.tile([P, 512], F32, name="warm", tag="tp")
+        warm_up(warm_bank, 9)
         pv_bank = acc_pool.tile([P, 512], F32, name="pv_bank", tag="acc")
         nc.tensor.transpose(pv_bank[:, 0:P], vrows[:].bitcast(F32), ident[:])
         nc.vector.tensor_copy(out=pv[:], in_=pv_bank[:, 0:P])
-        for q in range(PIECES):
-            spread_bias(q, q == 1)
-
-        state = {"ps": 0, "t": 0, "q": 0, "load": RAW_BUFS}
-
-        def next_prescale():
-            prescale_unit(state["ps"])
-            if state["load"] < UNITS:
-                load_unit(state["load"])
-                state["load"] += 1
-            state["ps"] += 1
-
-        def next_transpose():
-            while state["ps"] <= state["t"]:
-                next_prescale()
-            transpose_unit(state["t"])
-            state["t"] += 1
-
-        def next_quantise():
-            quantise_unit(state["q"])
-            state["q"] += 1
-
-        next_transpose()
-        transpose_x(0, True)
-        next_quantise()
-        transpose_x(1, True)
+        split_x(0)
+        warm_up(warm_bank, 2)
+        spread_bias(0, False)
+        transpose_x(0, dummies=1)
+        prescale(0, 0)
+        spread_bias(1, True)
+        transpose_pass(0, 0, 1)
+        transpose_pass(0, 1, 1)
+        prescale(0, 1)
         quantise_x(0)
+        split_x(1)
+        spread_bias(2, False)
+        transpose_pass(0, 2, 1)
+        transpose_pass(0, 3, 1)
+        quantise(0, 0, 2)
+        spread_bias(3, True)
+        split_x(2)
+        transpose_x(1, dummies=1)
+        quantise(0, 2, 4)
+        multiply(0, 0)
+        transpose_x(2)
         quantise_x(1)
-        next_prescale()
-        transpose_x(2, False)
+        split_x(3)
+        prescale_unit(1)
+        multiply(0, 1)
+        transpose_x(3)
         quantise_x(2)
-        transpose_x(3, False)
+        multiply(0, 2)
+        transpose_unit(1)
         quantise_x(3)
-        next_prescale()
-        multiply_unit(0, 0)
-        for k in range(UNITS + 1):
-            lead = 2 if k == 0 else k + 3
-            while state["t"] < min(UNITS, lead):
-                next_transpose()
-            while state["ps"] < min(UNITS, state["t"] + 1):
-                next_prescale()
-            if k >= 1:
-                finish_unit(k - 1)
-            while state["q"] < min(UNITS, state["t"], k + 3):
-                next_quantise()
-            if k < UNITS:
-                if k > 0:
-                    multiply_unit(k, 0)
-                multiply_unit(k, 1)
+        prescale_unit(2)
+        multiply(0, 3)
+        finish(0, 0)
+        quantise(1, 0, 4)
+        finish(0, 1)
+        transpose_unit(2)
+        spread_bias(4, False)
+        spread_bias(5, False)
+        prescale_unit(3)
+
+        loads = RAW_BUFS
+        for i in range(1, UNITS):
+            multiply(i, 0)
+            multiply(i, 1)
+            multiply(i, 2)
+            multiply(i, 3)
+            if loads < UNITS:
+                load_unit(loads)
+                loads += 1
+            if i + 1 < UNITS:
+                quantise(i + 1, 0, 4)
+            if i + 2 < UNITS:
+                transpose_unit(i + 2)
+            if i + 3 < UNITS:
+                prescale_unit(i + 3)
+            finish(i, 0)
+            finish(i, 1)

@@ -24,6 +24,8 @@ UNIT = 256
 UNITS = N // UNIT
 PIECE = 1024
 PIECES = (N + PIECE - 1) // PIECE
+FIRST_ROWS = 16
+REST_ROWS = 8
 BIAS_ROW = 32
 RAW_BUFS = 7
 GROUP_SIZES = (4, 4, 4, 4, 2, 2, 1, 1)
@@ -62,13 +64,14 @@ def tile_unicorelinearfp4_kernel(tc, x, weight, wscales, bias, out):
 
         ident = const.tile([P, P], F32, name="ident")
         zeros = const.tile([P, 512], BF16, name="zeros")
+        scratch = const.tile([P, 2], BF16, name="scratch")
         vrows = const.tile([P, UNIT], BF16, name="vrows")
-        pv = const.tile([P, P], F32, name="pv")
+        vcols = const.tile([P, P], F32, name="vcols")
         bias_sb = const.tile([P, N], BF16, name="bias_sb")
         xraw = const.tile([P, MT, K], BF16, name="xraw")
         xcodes = const.tile([P, MT, PASSES * P], U32, name="xcodes", align_bytes=64)
         xplane = const.tile([P, MT, PASSES * P], U8, name="xplane", align_bytes=64)
-        ws_pp = pv[:, 0:UNITS].bitcast(BF16)
+        ws_cols = vcols[:, 0:32].bitcast(BF16)
 
         raw = {}
         scl = {}
@@ -83,13 +86,16 @@ def tile_unicorelinearfp4_kernel(tc, x, weight, wscales, bias, out):
             for r in range(n):
                 nc.tensor.matmul(bank[:], lhsT=zeros[:, 0:P], rhs=zeros[:], start=True, stop=True)
 
+        def vector_row(i):
+            return i if i < FIRST_ROWS else i + FIRST_ROWS + REST_ROWS - UNITS
+
         def spread_bias(q, on_vector):
             units = min(4, UNITS - 4 * q)
-            bank = acc_pool.tile([P, 512], F32, name="sp%d" % q, tag="acc")
+            bank = tp_pool.tile([P, 512], F32, name="sp%d" % q, tag="tp")
             for u in range(units):
-                r = BIAS_ROW + 4 * q + u
+                r = BIAS_ROW + vector_row(4 * q + u)
                 nc.tensor.transpose(
-                    bank[:, u * P : (u + 1) * P], pv[:, r : r + 1].to_broadcast([P, P]), ident[:]
+                    bank[:, u * P : (u + 1) * P], vcols[:, r : r + 1].to_broadcast([P, P]), ident[:]
                 )
             words = bias_sb[:, q * PIECE : q * PIECE + units * UNIT].bitcast(F32)
             if on_vector:
@@ -119,10 +125,11 @@ def tile_unicorelinearfp4_kernel(tc, x, weight, wscales, bias, out):
             if i not in scl:
                 scl[i] = scl_pool.tile([P, n, 2, K // n], BF16, name="scl%d" % i, tag="scl")
             for j in range(2):
+                c = 2 * vector_row(i) + j
                 nc.vector.tensor_scalar(
                     out=scl[i][:, a, j, :].rearrange("p (u w e) -> p u w e", u=2, e=2),
                     in0=raw[i][:, a, j, :].rearrange("p (w u e) -> p u w e", u=2, e=2),
-                    scalar1=ws_pp[:, 2 * i + j : 2 * i + j + 1],
+                    scalar1=ws_cols[:, c : c + 1],
                     scalar2=None,
                     op0=MULT,
                 )
@@ -232,13 +239,15 @@ def tile_unicorelinearfp4_kernel(tc, x, weight, wscales, bias, out):
         def quantise_x(m):
             nc.vector.quantize_mx(out=xcodes[:, m, :].bitcast(FP8X4), scales=xplane[:, m, :], in_=xg[m][:])
 
-        nc.vector.memset(zeros[:].bitcast(I32), 0)
         nc.vector.memset(vrows[:].bitcast(I32), 0)
+        nc.vector.memset(zeros[:].bitcast(I32), 0)
+        nc.scalar.copy(out=scratch[:, 1:2], in_=zeros[:, 0:1])
         make_identity(nc, ident[:])
-        nc.scalar.dma_start(out=vrows[0:UNITS, :], in_=ws_vec.rearrange("(r n) -> r n", n=UNIT))
-        nc.scalar.dma_start(
-            out=vrows[BIAS_ROW : BIAS_ROW + UNITS, :], in_=bias_vec.rearrange("(r n) -> r n", n=UNIT)
-        )
+        for row, vec in ((0, ws_vec), (BIAS_ROW, bias_vec)):
+            rows = vec.rearrange("(r n) -> r n", n=UNIT)
+            nc.sync.dma_start(out=vrows[row : row + FIRST_ROWS, :], in_=rows[0:FIRST_ROWS, :])
+            rest = row + FIRST_ROWS
+            nc.sync.dma_start(out=vrows[rest : rest + REST_ROWS, :], in_=rows[UNITS - REST_ROWS : UNITS, :])
         nc.sync.dma_start(out=xraw[:, 0, :], in_=x_rows[:, 0, :])
         load_unit(0)
         for m in range(1, MT):
@@ -246,55 +255,57 @@ def tile_unicorelinearfp4_kernel(tc, x, weight, wscales, bias, out):
         for i in range(1, RAW_BUFS):
             load_unit(i)
 
-        warm_bank = tp_pool.tile([P, 512], F32, name="warm", tag="tp")
-        warm_up(warm_bank, 9)
-        pv_bank = acc_pool.tile([P, 512], F32, name="pv_bank", tag="acc")
-        nc.tensor.transpose(pv_bank[:, 0:P], vrows[:].bitcast(F32), ident[:])
-        nc.vector.tensor_copy(out=pv[:], in_=pv_bank[:, 0:P])
+        warm_bank = acc_pool.tile([P, 512], F32, name="warm", tag="acc")
+        warm_up(warm_bank, 6)
+        col_bank = acc_pool.tile([P, 512], F32, name="col_bank", tag="acc")
+        nc.tensor.transpose(col_bank[:, 0:P], vrows[:].bitcast(F32), ident[:])
+        nc.vector.tensor_copy(out=vcols[:], in_=col_bank[:, 0:P])
         split_x(0)
-        warm_up(warm_bank, 2)
+        warm_up(warm_bank, 1)
         spread_bias(0, False)
+        spread_bias(1, False)
         transpose_x(0, dummies=1)
         prescale(0, 0)
-        spread_bias(1, True)
         transpose_pass(0, 0, 1)
         transpose_pass(0, 1, 1)
         prescale(0, 1)
         quantise_x(0)
         split_x(1)
-        spread_bias(2, False)
         transpose_pass(0, 2, 1)
         transpose_pass(0, 3, 1)
-        quantise(0, 0, 2)
-        spread_bias(3, True)
         split_x(2)
+        quantise(0, 0, 2)
         transpose_x(1, dummies=1)
         quantise(0, 2, 4)
         multiply(0, 0)
         transpose_x(2)
-        quantise_x(1)
         split_x(3)
+        quantise_x(1)
+        transpose_x(3)
         prescale_unit(1)
         multiply(0, 1)
-        transpose_x(3)
         quantise_x(2)
-        multiply(0, 2)
-        transpose_unit(1)
+        transpose_pass(1, 0)
+        transpose_pass(1, 1)
         quantise_x(3)
+        multiply(0, 2)
+        transpose_pass(1, 2)
+        transpose_pass(1, 3)
         prescale_unit(2)
-        multiply(0, 3)
         finish(0, 0)
+        multiply(0, 3)
         quantise(1, 0, 4)
         finish(0, 1)
-        transpose_unit(2)
-        spread_bias(4, False)
-        spread_bias(5, False)
         prescale_unit(3)
+        transpose_unit(2)
+        spread_bias(2, False)
 
         loads = RAW_BUFS
         for i in range(1, UNITS):
             multiply(i, 0)
             multiply(i, 1)
+            if 2 + i < PIECES:
+                spread_bias(2 + i, False)
             multiply(i, 2)
             multiply(i, 3)
             if loads < UNITS:

@@ -127,8 +127,8 @@ def tile_unicorelinearfp4_kernel(tc, x, weight, wscales, bias, out):
             for j in range(2):
                 c = 2 * vector_row(i) + j
                 nc.vector.tensor_scalar(
-                    out=scl[i][:, a, j, :].rearrange("p (u w e) -> p u w e", u=2, e=2),
-                    in0=raw[i][:, a, j, :].rearrange("p (w u e) -> p u w e", u=2, e=2),
+                    out=scl[i][:, a, j, :].rearrange("p (u w e) -> p u w e", u=2, e=16),
+                    in0=raw[i][:, a, j, :].rearrange("p (w u e) -> p u w e", u=2, e=16),
                     scalar1=ws_cols[:, c : c + 1],
                     scalar2=None,
                     op0=MULT,
@@ -214,8 +214,8 @@ def tile_unicorelinearfp4_kernel(tc, x, weight, wscales, bias, out):
         def split_x(m):
             xdei[m] = xdei_pool.tile([P, K], BF16, name="xdei%d" % m, tag="xdei")
             nc.vector.tensor_copy(
-                out=xdei[m][:].rearrange("p (u w e) -> p u w e", u=2, e=2),
-                in_=xraw[:, m, :].rearrange("p (w u e) -> p u w e", u=2, e=2),
+                out=xdei[m][:].rearrange("p (u w e) -> p u w e", u=2, e=16),
+                in_=xraw[:, m, :].rearrange("p (w u e) -> p u w e", u=2, e=16),
             )
 
         def transpose_x(m, engines="ss", dummies=0):

@@ -138,11 +138,10 @@ def tile_unicorelinearfp4_kernel(tc, x, weight, wscales, bias, out):
             for a in range(parts(i)):
                 prescale(i, a)
 
-        def transpose_pass(i, g, dummies=0):
+        def transpose_pass(i, g):
             if i not in grp:
                 grp[i] = grp_pool.tile([P, PASSES * 4 * UNIT], BF16, name="grp%d" % i, tag="grp", align_bytes=64)
             bank = tp_pool.tile([P, 512], F32, name="tp%d_%d" % (i, g), tag="tp")
-            warm_up(bank, dummies)
             per = PASSES // parts(i)
             for j in range(2):
                 words = scl[i][:, g // per, j, :].bitcast(F32)
@@ -218,12 +217,11 @@ def tile_unicorelinearfp4_kernel(tc, x, weight, wscales, bias, out):
                 in_=xraw[:, m, :].rearrange("p (w u e) -> p u w e", u=2, e=16),
             )
 
-        def transpose_x(m, engines="ss", dummies=0):
+        def transpose_x(m, engines="ss"):
             xg[m] = xg_pool.tile([P, PASSES * 4 * P], BF16, name="xg%d" % m, tag="xg", align_bytes=64)
             words = xdei[m][:].bitcast(F32)
             for b in range(2):
                 bank = tp_pool.tile([P, 512], F32, name="tpx%d_%d" % (m, b), tag="tp")
-                warm_up(bank, dummies)
                 for s in range(4):
                     blk = PASSES * (s % 2) + 2 * b + s // 2
                     nc.tensor.transpose(
@@ -264,18 +262,18 @@ def tile_unicorelinearfp4_kernel(tc, x, weight, wscales, bias, out):
         warm_up(warm_bank, 1)
         spread_bias(0, False)
         spread_bias(1, False)
-        transpose_x(0, dummies=1)
+        transpose_x(0)
         prescale(0, 0)
-        transpose_pass(0, 0, 1)
-        transpose_pass(0, 1, 1)
+        transpose_pass(0, 0)
+        transpose_pass(0, 1)
         prescale(0, 1)
         quantise_x(0)
         split_x(1)
-        transpose_pass(0, 2, 1)
-        transpose_pass(0, 3, 1)
+        transpose_pass(0, 2)
+        transpose_pass(0, 3)
         split_x(2)
         quantise(0, 0, 2)
-        transpose_x(1, dummies=1)
+        transpose_x(1)
         quantise(0, 2, 4)
         multiply(0, 0)
         transpose_x(2)

@@ -89,19 +89,20 @@ def tile_unicorelinearfp4_kernel(tc, x, weight, wscales, bias, out):
         def vector_row(i):
             return i if i < FIRST_ROWS else i + FIRST_ROWS + REST_ROWS - UNITS
 
-        def spread_bias(q, on_vector):
-            units = min(4, UNITS - 4 * q)
-            bank = tp_pool.tile([P, 512], F32, name="sp%d" % q, tag="tp")
-            for u in range(units):
+        spread = {}
+
+        def spread_bias(q, pool, tag):
+            spread[q] = pool.tile([P, 512], F32, name="sp%d" % q, tag=tag)
+            for u in range(min(4, UNITS - 4 * q)):
                 r = BIAS_ROW + vector_row(4 * q + u)
                 nc.tensor.transpose(
-                    bank[:, u * P : (u + 1) * P], vcols[:, r : r + 1].to_broadcast([P, P]), ident[:]
+                    spread[q][:, u * P : (u + 1) * P], vcols[:, r : r + 1].to_broadcast([P, P]), ident[:]
                 )
-            words = bias_sb[:, q * PIECE : q * PIECE + units * UNIT].bitcast(F32)
-            if on_vector:
-                nc.vector.tensor_copy(out=words, in_=bank[:, 0 : units * P])
-            else:
-                nc.scalar.copy(out=words, in_=bank[:, 0 : units * P])
+
+        def keep_bias(q):
+            words = min(4, UNITS - 4 * q) * P
+            cols = slice(q * PIECE, q * PIECE + 2 * words)
+            nc.scalar.copy(out=bias_sb[:, cols].bitcast(F32), in_=spread[q][:, 0:words])
 
         def unit_rows(i):
             return weight[i * UNIT : (i + 1) * UNIT, :].rearrange("(p j) k -> p j k", j=2)
@@ -138,10 +139,15 @@ def tile_unicorelinearfp4_kernel(tc, x, weight, wscales, bias, out):
             for a in range(parts(i)):
                 prescale(i, a)
 
+        def soften(bank):
+            nc.tensor.matmul(bank[:, 0:64], lhsT=zeros[:, 0:P], rhs=zeros[:, 0:64], start=True, stop=True)
+
         def transpose_pass(i, g):
             if i not in grp:
                 grp[i] = grp_pool.tile([P, PASSES * 4 * UNIT], BF16, name="grp%d" % i, tag="grp", align_bytes=64)
             bank = tp_pool.tile([P, 512], F32, name="tp%d_%d" % (i, g), tag="tp")
+            if i > 2 and g == 0:
+                soften(bank)
             per = PASSES // parts(i)
             for j in range(2):
                 words = scl[i][:, g // per, j, :].bitcast(F32)
@@ -175,6 +181,8 @@ def tile_unicorelinearfp4_kernel(tc, x, weight, wscales, bias, out):
             b = m // 2
             if (i, b) not in acc:
                 acc[(i, b)] = acc_pool.tile([P, 512], F32, name="acc%d_%d" % (i, b), tag="acc")
+                if i > 0 and b == 0:
+                    soften(acc[(i, b)])
             for g in range(PASSES):
                 nc.tensor.matmul_mx(
                     out=acc[(i, b)][:, (m % 2) * UNIT : (m % 2 + 1) * UNIT],
@@ -198,12 +206,7 @@ def tile_unicorelinearfp4_kernel(tc, x, weight, wscales, bias, out):
                 in1=row,
                 op=ADD,
             )
-            if i == UNITS - 1:
-                nc.sync.dma_start(
-                    out=out_rows[:, 2 * b : 2 * b + 2, i * UNIT : (i + 1) * UNIT],
-                    in_=stage[gi][:, 2 * b : 2 * b + 2, off : off + UNIT],
-                )
-            elif b == 1 and i == group_start[gi] + GROUP_SIZES[gi] - 1:
+            if b == 1 and i == group_start[gi] + GROUP_SIZES[gi] - 1:
                 a = group_start[gi] * UNIT
                 w = GROUP_SIZES[gi] * UNIT
                 nc.sync.dma_start(out=out_rows[:, :, a : a + w], in_=stage[gi][:, :, 0:w])
@@ -216,6 +219,19 @@ def tile_unicorelinearfp4_kernel(tc, x, weight, wscales, bias, out):
                 out=xdei[m][:].rearrange("p (u w e) -> p u w e", u=2, e=16),
                 in_=xraw[:, m, :].rearrange("p (w u e) -> p u w e", u=2, e=16),
             )
+
+        def finish_last(m):
+            i = UNITS - 1
+            gi = group_of[i]
+            if gi not in stage:
+                stage[gi] = stage_pool.tile([P, MT, 4 * UNIT], F32, name="stage%d" % gi, tag="stage")
+            nc.vector.tensor_tensor(
+                out=stage[gi][:, m, 0:UNIT],
+                in0=acc[(i, m // 2)][:, (m % 2) * UNIT : (m % 2 + 1) * UNIT],
+                in1=bias_sb[:, i * UNIT : (i + 1) * UNIT],
+                op=ADD,
+            )
+            nc.sync.dma_start(out=out_rows[:, m, i * UNIT : (i + 1) * UNIT], in_=stage[gi][:, m, 0:UNIT])
 
         def transpose_x(m, engines="ss"):
             xg[m] = xg_pool.tile([P, PASSES * 4 * P], BF16, name="xg%d" % m, tag="xg", align_bytes=64)
@@ -260,8 +276,8 @@ def tile_unicorelinearfp4_kernel(tc, x, weight, wscales, bias, out):
         nc.vector.tensor_copy(out=vcols[:], in_=col_bank[:, 0:P])
         split_x(0)
         warm_up(warm_bank, 1)
-        spread_bias(0, False)
-        spread_bias(1, False)
+        spread_bias(0, acc_pool, "acc")
+        spread_bias(1, acc_pool, "acc")
         transpose_x(0)
         prescale(0, 0)
         transpose_pass(0, 0)
@@ -274,6 +290,8 @@ def tile_unicorelinearfp4_kernel(tc, x, weight, wscales, bias, out):
         split_x(2)
         quantise(0, 0, 2)
         transpose_x(1)
+        keep_bias(0)
+        keep_bias(1)
         quantise(0, 2, 4)
         multiply(0, 0)
         transpose_x(2)
@@ -296,24 +314,31 @@ def tile_unicorelinearfp4_kernel(tc, x, weight, wscales, bias, out):
         finish(0, 1)
         prescale_unit(3)
         transpose_unit(2)
-        spread_bias(2, False)
+        spread_bias(2, tp_pool, "tp")
+        keep_bias(2)
 
         loads = RAW_BUFS
         for i in range(1, UNITS):
-            multiply(i, 0)
-            multiply(i, 1)
-            if 2 + i < PIECES:
-                spread_bias(2 + i, False)
-            multiply(i, 2)
-            multiply(i, 3)
+            for m in range(MT):
+                multiply(i, m)
+                if m == 1 and 2 + i < PIECES:
+                    spread_bias(2 + i, tp_pool, "tp")
+                    keep_bias(2 + i)
             if loads < UNITS:
                 load_unit(loads)
                 loads += 1
-            if i + 1 < UNITS:
+            if i + 1 < UNITS - 1:
                 quantise(i + 1, 0, 4)
+            elif i + 1 < UNITS:
+                quantise(i + 1, 0, 2)
+                quantise(i + 1, 2, 4)
             if i + 2 < UNITS:
                 transpose_unit(i + 2)
             if i + 3 < UNITS:
                 prescale_unit(i + 3)
-            finish(i, 0)
-            finish(i, 1)
+            if i < UNITS - 1:
+                finish(i, 0)
+                finish(i, 1)
+            else:
+                for m in range(MT):
+                    finish_last(m)

@@ -139,15 +139,10 @@ def tile_unicorelinearfp4_kernel(tc, x, weight, wscales, bias, out):
             for a in range(parts(i)):
                 prescale(i, a)
 
-        def soften(bank):
-            nc.tensor.matmul(bank[:, 0:64], lhsT=zeros[:, 0:P], rhs=zeros[:, 0:64], start=True, stop=True)
-
         def transpose_pass(i, g):
             if i not in grp:
                 grp[i] = grp_pool.tile([P, PASSES * 4 * UNIT], BF16, name="grp%d" % i, tag="grp", align_bytes=64)
             bank = tp_pool.tile([P, 512], F32, name="tp%d_%d" % (i, g), tag="tp")
-            if i > 2 and g == 0:
-                soften(bank)
             per = PASSES // parts(i)
             for j in range(2):
                 words = scl[i][:, g // per, j, :].bitcast(F32)
@@ -181,8 +176,6 @@ def tile_unicorelinearfp4_kernel(tc, x, weight, wscales, bias, out):
             b = m // 2
             if (i, b) not in acc:
                 acc[(i, b)] = acc_pool.tile([P, 512], F32, name="acc%d_%d" % (i, b), tag="acc")
-                if i > 0 and b == 0:
-                    soften(acc[(i, b)])
             for g in range(PASSES):
                 nc.tensor.matmul_mx(
                     out=acc[(i, b)][:, (m % 2) * UNIT : (m % 2 + 1) * UNIT],

@@ -10,6 +10,7 @@ U32 = mybir.dt.uint32
 U8 = mybir.dt.uint8
 I32 = mybir.dt.int32
 MULT = mybir.AluOpType.mult
+COPY = mybir.ActivationFunctionType.Copy
 ADD = mybir.AluOpType.add
 
 P = 128
@@ -28,8 +29,9 @@ FIRST_ROWS = 16
 REST_ROWS = 8
 BIAS_ROW = 32
 RAW_BUFS = 7
-GROUP_SIZES = (4, 4, 4, 4, 2, 2, 1, 1)
-HALF = K // 2
+GROUP_SIZES = (2,) * 9 + (1,) * 4
+TURNED = (12, 19)
+CHUNK = 8
 
 
 def tile_unicorelinearfp4_kernel(tc, x, weight, wscales, bias, out):
@@ -54,10 +56,13 @@ def tile_unicorelinearfp4_kernel(tc, x, weight, wscales, bias, out):
         xdei_pool = ctx.enter_context(tc.tile_pool(name="xdei", bufs=2))
         xg_pool = ctx.enter_context(tc.tile_pool(name="xg", bufs=2))
         raw_pool = ctx.enter_context(tc.tile_pool(name="raw", bufs=RAW_BUFS))
+        turn_pool = ctx.enter_context(tc.tile_pool(name="turn", bufs=1))
+        sclt_pool = ctx.enter_context(tc.tile_pool(name="sclt", bufs=4))
+        rawt_pool = ctx.enter_context(tc.tile_pool(name="rawt", bufs=1))
         scl_pool = ctx.enter_context(tc.tile_pool(name="scl", bufs=3))
         grp_pool = ctx.enter_context(tc.tile_pool(name="grp", bufs=3))
         code_pool = ctx.enter_context(tc.tile_pool(name="code", bufs=4))
-        stage_pool = ctx.enter_context(tc.tile_pool(name="stage", bufs=3))
+        stage_pool = ctx.enter_context(tc.tile_pool(name="stage", bufs=4))
         tp_pool = ctx.enter_context(tc.psum_pool(name="tp", bufs=4))
         acc_pool = ctx.enter_context(tc.psum_pool(name="acc", bufs=4))
         ctx.enter_context(tc.manual_schedule())
@@ -71,6 +76,8 @@ def tile_unicorelinearfp4_kernel(tc, x, weight, wscales, bias, out):
         xraw = const.tile([P, MT, K], BF16, name="xraw")
         xcodes = const.tile([P, MT, PASSES * P], U32, name="xcodes", align_bytes=64)
         xplane = const.tile([P, MT, PASSES * P], U8, name="xplane", align_bytes=64)
+        ws_turn = const.tile([P, len(TURNED), 2 * CHUNK], BF16, name="ws_turn")
+        ws_turn_f32 = const.tile([P, len(TURNED), CHUNK], F32, name="ws_turn_f32")
         ws_cols = vcols[:, 0:32].bitcast(BF16)
 
         raw = {}
@@ -108,8 +115,51 @@ def tile_unicorelinearfp4_kernel(tc, x, weight, wscales, bias, out):
             return weight[i * UNIT : (i + 1) * UNIT, :].rearrange("(p j) k -> p j k", j=2)
 
         def load_unit(i):
-            for a in range(parts(i)):
-                load_part(i, a)
+            if i not in TURNED:
+                for a in range(parts(i)):
+                    load_part(i, a)
+
+        def load_turned(i, h):
+            if i not in raw:
+                raw[i] = rawt_pool.tile([P, 4 * CHUNK, P], BF16, name="raw%d" % i, tag="rawt")
+            src = weight.rearrange("n k -> (n k)")[i * UNIT * K : (i + 1) * UNIT * K].rearrange(
+                "(b r s k) -> b r s k", r=4 * CHUNK, s=4, k=P
+            )
+            rows = slice(2 * CHUNK * h, 2 * CHUNK * (h + 1))
+            for q in range(4):
+                nc.sync.dma_start(out=raw[i][32 * q : 32 * q + 32, rows, :], in_=src[:, rows, q, :])
+
+        def load_ws_turned():
+            src = ws_vec.rearrange("(i b c) -> b i c", b=32, c=CHUNK)[:, TURNED[0] : TURNED[-1] + 1 : TURNED[1] - TURNED[0], :]
+            for q in range(4):
+                nc.sync.dma_start(out=ws_turn[32 * q : 32 * q + 32, :, 0:CHUNK], in_=src)
+
+        chunk = {}
+        turned = {}
+
+        def prescale_turned(i, c):
+            w = 2 * K // CHUNK
+            chunk[(i, c)] = sclt_pool.tile([P, w], BF16, name="sclt%d_%d" % (i, c), tag="sclt", align_bytes=64)
+            nc.scalar.activation(
+                out=chunk[(i, c)][:].rearrange("p (u w e) -> p u w e", u=2, e=16),
+                in_=raw[i][:].rearrange("p r k -> p (r k)")[:, c * w : (c + 1) * w].rearrange("p (w u e) -> p u w e", u=2, e=16),
+                func=COPY,
+                scale=ws_turn_f32[:, TURNED.index(i), c : c + 1],
+            )
+
+        def turn(i, c):
+            if i not in turned:
+                turned[i] = turn_pool.tile([P, K], F32, name="turn%d" % i, tag="turn", align_bytes=64)
+            w = K // CHUNK
+            nc.vector.transpose(out=turned[i][:, c * w : (c + 1) * w], in_=chunk[(i, c)][:].bitcast(F32))
+
+        def interleave(i):
+            grp[i] = grp_pool.tile([P, PASSES * 4 * UNIT], BF16, name="grp%d" % i, tag="grp", align_bytes=64)
+            for g in range(PASSES):
+                nc.scalar.copy(
+                    out=grp[i][:, g * 1024 : (g + 1) * 1024].bitcast(F32).rearrange("p (c b u) -> p c b u", c=CHUNK, u=2),
+                    in_=turned[i][:].rearrange("p (c u g b) -> p g c b u", c=CHUNK, u=2, g=4)[:, g, :, :, :],
+                )
 
         def parts(i):
             return 2 if i == 0 else 1
@@ -124,7 +174,7 @@ def tile_unicorelinearfp4_kernel(tc, x, weight, wscales, bias, out):
         def prescale(i, a):
             n = parts(i)
             if i not in scl:
-                scl[i] = scl_pool.tile([P, n, 2, K // n], BF16, name="scl%d" % i, tag="scl")
+                scl[i] = scl_pool.tile([P, n, 2, K // n], BF16, name="scl%d" % i, tag="scl", align_bytes=64)
             for j in range(2):
                 c = 2 * vector_row(i) + j
                 nc.vector.tensor_scalar(
@@ -139,7 +189,9 @@ def tile_unicorelinearfp4_kernel(tc, x, weight, wscales, bias, out):
             for a in range(parts(i)):
                 prescale(i, a)
 
-        def transpose_pass(i, g):
+        wbank = {}
+
+        def transpose_pass(i, g, copy):
             if i not in grp:
                 grp[i] = grp_pool.tile([P, PASSES * 4 * UNIT], BF16, name="grp%d" % i, tag="grp", align_bytes=64)
             bank = tp_pool.tile([P, 512], F32, name="tp%d_%d" % (i, g), tag="tp")
@@ -152,14 +204,19 @@ def tile_unicorelinearfp4_kernel(tc, x, weight, wscales, bias, out):
                     nc.tensor.transpose(
                         bank[:, s * P : (s + 1) * P], words[:, blk * P : (blk + 1) * P], ident[:]
                     )
-            nc.scalar.copy(
+            wbank[(i, g)] = bank
+            if copy is not None:
+                copy_pass(i, g, copy)
+
+        def copy_pass(i, g, copy):
+            copy(
                 out=grp[i][:, g * 1024 : (g + 1) * 1024].bitcast(F32).rearrange("p (c s) -> p c s", s=4),
-                in_=bank[:].rearrange("p (s c) -> p c s", s=4),
+                in_=wbank[(i, g)][:].rearrange("p (s c) -> p c s", s=4),
             )
 
         def transpose_unit(i):
             for g in range(PASSES):
-                transpose_pass(i, g)
+                transpose_pass(i, g, nc.scalar.copy)
 
         def quantise(i, g0, g1):
             if i not in codes:
@@ -190,15 +247,16 @@ def tile_unicorelinearfp4_kernel(tc, x, weight, wscales, bias, out):
         def finish(i, b):
             gi = group_of[i]
             if gi not in stage:
-                stage[gi] = stage_pool.tile([P, MT, 4 * UNIT], F32, name="stage%d" % gi, tag="stage")
+                stage[gi] = stage_pool.tile([P, MT, 2 * UNIT], F32, name="stage%d" % gi, tag="stage")
             off = (i - group_start[gi]) * UNIT
             row = bias_sb[:, i * UNIT : (i + 1) * UNIT].unsqueeze(1).to_broadcast([P, 2, UNIT])
-            nc.vector.tensor_tensor(
-                out=stage[gi][:, 2 * b : 2 * b + 2, off : off + UNIT],
-                in0=acc[(i, b)][:].rearrange("p (m n) -> p m n", m=2),
-                in1=row,
-                op=ADD,
-            )
+            result = stage[gi][:, 2 * b : 2 * b + 2, off : off + UNIT]
+            product = acc[(i, b)][:].rearrange("p (m n) -> p m n", m=2)
+            if i in TURNED:
+                row = row.rearrange("p m (b c) -> p m b c", c=CHUNK)
+                result = result.rearrange("p m (b c) -> p m b c", c=CHUNK)
+                product = acc[(i, b)][:].rearrange("p (m c b) -> p m b c", m=2, c=CHUNK)
+            nc.vector.tensor_tensor(out=result, in0=product, in1=row, op=ADD)
             if b == 1 and i == group_start[gi] + GROUP_SIZES[gi] - 1:
                 a = group_start[gi] * UNIT
                 w = GROUP_SIZES[gi] * UNIT
@@ -217,7 +275,7 @@ def tile_unicorelinearfp4_kernel(tc, x, weight, wscales, bias, out):
             i = UNITS - 1
             gi = group_of[i]
             if gi not in stage:
-                stage[gi] = stage_pool.tile([P, MT, 4 * UNIT], F32, name="stage%d" % gi, tag="stage")
+                stage[gi] = stage_pool.tile([P, MT, 2 * UNIT], F32, name="stage%d" % gi, tag="stage")
             nc.vector.tensor_tensor(
                 out=stage[gi][:, m, 0:UNIT],
                 in0=acc[(i, m // 2)][:, (m % 2) * UNIT : (m % 2 + 1) * UNIT],
@@ -226,26 +284,29 @@ def tile_unicorelinearfp4_kernel(tc, x, weight, wscales, bias, out):
             )
             nc.sync.dma_start(out=out_rows[:, m, i * UNIT : (i + 1) * UNIT], in_=stage[gi][:, m, 0:UNIT])
 
-        def transpose_x(m, engines="ss"):
-            xg[m] = xg_pool.tile([P, PASSES * 4 * P], BF16, name="xg%d" % m, tag="xg", align_bytes=64)
+        xbank = {}
+
+        def transpose_x(m, b):
+            xbank[(m, b)] = tp_pool.tile([P, 512], F32, name="tpx%d_%d" % (m, b), tag="tp")
             words = xdei[m][:].bitcast(F32)
-            for b in range(2):
-                bank = tp_pool.tile([P, 512], F32, name="tpx%d_%d" % (m, b), tag="tp")
-                for s in range(4):
-                    blk = PASSES * (s % 2) + 2 * b + s // 2
-                    nc.tensor.transpose(
-                        bank[:, s * P : (s + 1) * P], words[:, blk * P : (blk + 1) * P], ident[:]
-                    )
-                dst = xg[m][:, b * 1024 : (b + 1) * 1024].bitcast(F32).rearrange("p (g c h) -> p g c h", g=2, h=2)
-                src = bank[:].rearrange("p (g h c) -> p g c h", g=2, h=2)
-                if engines[b] == "v":
-                    nc.vector.tensor_copy(out=dst, in_=src)
-                else:
-                    nc.scalar.copy(out=dst, in_=src)
+            for s in range(4):
+                blk = PASSES * (s % 2) + 2 * b + s // 2
+                nc.tensor.transpose(
+                    xbank[(m, b)][:, s * P : (s + 1) * P], words[:, blk * P : (blk + 1) * P], ident[:]
+                )
+
+        def copy_x(m, b, copy):
+            if m not in xg:
+                xg[m] = xg_pool.tile([P, PASSES * 4 * P], BF16, name="xg%d" % m, tag="xg", align_bytes=64)
+            copy(
+                out=xg[m][:, b * 1024 : (b + 1) * 1024].bitcast(F32).rearrange("p (g c h) -> p g c h", g=2, h=2),
+                in_=xbank[(m, b)][:].rearrange("p (g h c) -> p g c h", g=2, h=2),
+            )
 
         def quantise_x(m):
             nc.vector.quantize_mx(out=xcodes[:, m, :].bitcast(FP8X4), scales=xplane[:, m, :], in_=xg[m][:])
 
+        nc.sync.dma_start(out=xraw[:, 0, :], in_=x_rows[:, 0, :])
         nc.vector.memset(vrows[:].bitcast(I32), 0)
         nc.vector.memset(zeros[:].bitcast(I32), 0)
         nc.scalar.copy(out=scratch[:, 1:2], in_=zeros[:, 0:1])
@@ -255,7 +316,6 @@ def tile_unicorelinearfp4_kernel(tc, x, weight, wscales, bias, out):
             nc.sync.dma_start(out=vrows[row : row + FIRST_ROWS, :], in_=rows[0:FIRST_ROWS, :])
             rest = row + FIRST_ROWS
             nc.sync.dma_start(out=vrows[rest : rest + REST_ROWS, :], in_=rows[UNITS - REST_ROWS : UNITS, :])
-        nc.sync.dma_start(out=xraw[:, 0, :], in_=x_rows[:, 0, :])
         load_unit(0)
         for m in range(1, MT):
             nc.sync.dma_start(out=xraw[:, m, :], in_=x_rows[:, m, :])
@@ -263,72 +323,112 @@ def tile_unicorelinearfp4_kernel(tc, x, weight, wscales, bias, out):
             load_unit(i)
 
         warm_bank = acc_pool.tile([P, 512], F32, name="warm", tag="acc")
-        warm_up(warm_bank, 6)
+        warm_up(warm_bank, 4)
         col_bank = acc_pool.tile([P, 512], F32, name="col_bank", tag="acc")
         nc.tensor.transpose(col_bank[:, 0:P], vrows[:].bitcast(F32), ident[:])
-        nc.vector.tensor_copy(out=vcols[:], in_=col_bank[:, 0:P])
         split_x(0)
-        warm_up(warm_bank, 1)
-        spread_bias(0, acc_pool, "acc")
-        spread_bias(1, acc_pool, "acc")
-        transpose_x(0)
+        nc.vector.tensor_copy(out=vcols[:], in_=col_bank[:, 0:P])
+        transpose_x(0, 0)
+        copy_x(0, 0, nc.scalar.copy)
+        transpose_x(0, 1)
         prescale(0, 0)
-        transpose_pass(0, 0)
-        transpose_pass(0, 1)
+        copy_x(0, 1, nc.vector.tensor_copy)
+        transpose_pass(0, 0, nc.scalar.copy)
+        transpose_pass(0, 1, nc.scalar.copy)
         prescale(0, 1)
         quantise_x(0)
         split_x(1)
-        transpose_pass(0, 2)
-        transpose_pass(0, 3)
-        split_x(2)
+        transpose_pass(0, 2, nc.scalar.copy)
+        transpose_pass(0, 3, nc.scalar.copy)
+        spread_bias(0, acc_pool, "acc")
+        spread_bias(1, acc_pool, "acc")
         quantise(0, 0, 2)
-        transpose_x(1)
-        keep_bias(0)
-        keep_bias(1)
+        transpose_x(1, 0)
+        copy_x(1, 0, nc.scalar.copy)
+        transpose_x(1, 1)
+        copy_x(1, 1, nc.scalar.copy)
+        split_x(2)
+        transpose_x(2, 0)
+        copy_x(2, 0, nc.scalar.copy)
+        transpose_x(2, 1)
+        copy_x(2, 1, nc.scalar.copy)
         quantise(0, 2, 4)
         multiply(0, 0)
-        transpose_x(2)
         split_x(3)
         quantise_x(1)
-        transpose_x(3)
-        prescale_unit(1)
+        transpose_x(3, 0)
+        copy_x(3, 0, nc.scalar.copy)
+        transpose_x(3, 1)
+        copy_x(3, 1, nc.scalar.copy)
         multiply(0, 1)
+        keep_bias(0)
         quantise_x(2)
-        transpose_pass(1, 0)
-        transpose_pass(1, 1)
-        quantise_x(3)
+        prescale_unit(1)
         multiply(0, 2)
-        transpose_pass(1, 2)
-        transpose_pass(1, 3)
-        prescale_unit(2)
-        finish(0, 0)
+        transpose_unit(1)
+        keep_bias(1)
+        quantise_x(3)
         multiply(0, 3)
-        quantise(1, 0, 4)
+        prescale_unit(2)
+        quantise(1, 0, 2)
+        quantise(1, 2, 4)
+        transpose_unit(2)
+        finish(0, 0)
         finish(0, 1)
         prescale_unit(3)
-        transpose_unit(2)
-        spread_bias(2, tp_pool, "tp")
-        keep_bias(2)
 
         loads = RAW_BUFS
+        lead = TURNED[0]
+        begin = {}
+        for v in TURNED:
+            begin[v] = v - 7
+
+        def run_unit(i):
+            return i + 2 if i + 2 < lead else i + 3
+
+        def chunks_of(v, i):
+            span = v - 3 - begin[v]
+            return [c for c in range(CHUNK) if begin[v] + c * span // CHUNK == i]
+
         for i in range(1, UNITS):
             for m in range(MT):
                 multiply(i, m)
-                if m == 1 and 2 + i < PIECES:
-                    spread_bias(2 + i, tp_pool, "tp")
-                    keep_bias(2 + i)
-            if loads < UNITS:
-                load_unit(loads)
+                if m == 1 and 2 * i < PIECES:
+                    for q in (2 * i, 2 * i + 1):
+                        spread_bias(q, tp_pool, "tp")
+                        keep_bias(q)
+            if i == 1:
+                load_ws_turned()
+            for v in TURNED:
+                for h in range(2):
+                    if i == max(1, begin[v] - 4 + 1 * h):
+                        load_turned(v, h)
+            while loads < UNITS and loads <= i + 10:
+                if loads not in TURNED:
+                    load_unit(loads)
                 loads += 1
-            if i + 1 < UNITS - 1:
-                quantise(i + 1, 0, 4)
-            elif i + 1 < UNITS:
-                quantise(i + 1, 0, 2)
-                quantise(i + 1, 2, 4)
-            if i + 2 < UNITS:
-                transpose_unit(i + 2)
-            if i + 3 < UNITS:
-                prescale_unit(i + 3)
+            if run_unit(i - 1) < UNITS - 1:
+                quantise(run_unit(i - 1), 0, 4)
+            elif run_unit(i - 1) < UNITS:
+                quantise(run_unit(i - 1), 0, 2)
+                quantise(run_unit(i - 1), 2, 4)
+            if i == lead - 2:
+                quantise(lead, 0, 4)
+            if i == begin[TURNED[0]] - 1:
+                for v in range(len(TURNED)):
+                    nc.vector.tensor_copy(out=ws_turn_f32[:, v, :], in_=ws_turn[:, v, 0:CHUNK])
+            for v in TURNED:
+                for c in chunks_of(v, i - 1):
+                    turn(v, c)
+            if run_unit(i) < UNITS and run_unit(i) not in TURNED:
+                transpose_unit(run_unit(i))
+            for v in TURNED:
+                if i == v - 3:
+                    interleave(v)
+                for c in chunks_of(v, i):
+                    prescale_turned(v, c)
+            if run_unit(i + 1) < UNITS and run_unit(i + 1) not in TURNED:
+                prescale_unit(run_unit(i + 1))
             if i < UNITS - 1:
                 finish(i, 0)
                 finish(i, 1)

from contextlib import ExitStack

import concourse.mybir as mybir
from concourse.masks import make_identity

FP8X4 = mybir.dt.float8_e4m3fn_x4
BF16 = mybir.dt.bfloat16
F32 = mybir.dt.float32
U32 = mybir.dt.uint32
U8 = mybir.dt.uint8
I32 = mybir.dt.int32
MULT = mybir.AluOpType.mult
COPY = mybir.ActivationFunctionType.Copy
ADD = mybir.AluOpType.add

P = 128
TOKENS = 512
K = 2048
N = 5632
FLOPS = 2 * TOKENS * K * N

PASSES = K // 512
MT = TOKENS // P
UNIT = 256
UNITS = N // UNIT
PIECE = 1024
PIECES = (N + PIECE - 1) // PIECE
FIRST_ROWS = 16
REST_ROWS = 8
BIAS_ROW = 32
RAW_BUFS = 7
GROUP_SIZES = (2,) * 9 + (1,) * 4
TURNED = (12, 19)
CHUNK = 8


def tile_unicorelinearfp4_kernel(tc, x, weight, wscales, bias, out):
    nc = tc.nc
    x_rows = x.flatten_outer_dims().rearrange("(p m) k -> p m k", m=MT)
    out_rows = out.flatten_outer_dims().rearrange("(p m) n -> p m n", m=MT)
    ws_vec = wscales.rearrange("n o -> (n o)")
    bias_vec = bias.rearrange("o n -> (o n)")

    group_of = {}
    group_start = []
    first = 0
    for gi, size in enumerate(GROUP_SIZES):
        group_start.append(first)
        for u in range(first, first + size):
            group_of[u] = gi
        first += size
    assert first == UNITS

    with ExitStack() as ctx:
        const = ctx.enter_context(tc.tile_pool(name="const", bufs=1))
        xdei_pool = ctx.enter_context(tc.tile_pool(name="xdei", bufs=2))
        xg_pool = ctx.enter_context(tc.tile_pool(name="xg", bufs=2))
        raw_pool = ctx.enter_context(tc.tile_pool(name="raw", bufs=RAW_BUFS))
        turn_pool = ctx.enter_context(tc.tile_pool(name="turn", bufs=1))
        sclt_pool = ctx.enter_context(tc.tile_pool(name="sclt", bufs=4))
        rawt_pool = ctx.enter_context(tc.tile_pool(name="rawt", bufs=1))
        scl_pool = ctx.enter_context(tc.tile_pool(name="scl", bufs=3))
        grp_pool = ctx.enter_context(tc.tile_pool(name="grp", bufs=3))
        code_pool = ctx.enter_context(tc.tile_pool(name="code", bufs=4))
        stage_pool = ctx.enter_context(tc.tile_pool(name="stage", bufs=4))
        tp_pool = ctx.enter_context(tc.psum_pool(name="tp", bufs=4))
        acc_pool = ctx.enter_context(tc.psum_pool(name="acc", bufs=4))
        ctx.enter_context(tc.manual_schedule())

        ident = const.tile([P, P], F32, name="ident")
        zeros = const.tile([P, 512], BF16, name="zeros")
        scratch = const.tile([P, 2], BF16, name="scratch")
        vrows = const.tile([P, UNIT], BF16, name="vrows")
        vcols = const.tile([P, P], F32, name="vcols")
        bias_sb = const.tile([P, N], BF16, name="bias_sb")
        xraw = const.tile([P, MT, K], BF16, name="xraw")
        xcodes = const.tile([P, MT, PASSES * P], U32, name="xcodes", align_bytes=64)
        xplane = const.tile([P, MT, PASSES * P], U8, name="xplane", align_bytes=64)
        ws_turn = const.tile([P, len(TURNED), 2 * CHUNK], BF16, name="ws_turn")
        ws_turn_f32 = const.tile([P, len(TURNED), CHUNK], F32, name="ws_turn_f32")
        ws_cols = vcols[:, 0:32].bitcast(BF16)

        raw = {}
        scl = {}
        grp = {}
        codes = {}
        plane = {}
        acc = {}
        stage = {}
        xg = {}

        def warm_up(bank, n):
            for r in range(n):
                nc.tensor.matmul(bank[:], lhsT=zeros[:, 0:P], rhs=zeros[:], start=True, stop=True)

        def vector_row(i):
            return i if i < FIRST_ROWS else i + FIRST_ROWS + REST_ROWS - UNITS

        spread = {}

        def spread_bias(q, pool, tag):
            spread[q] = pool.tile([P, 512], F32, name="sp%d" % q, tag=tag)
            for u in range(min(4, UNITS - 4 * q)):
                r = BIAS_ROW + vector_row(4 * q + u)
                nc.tensor.transpose(
                    spread[q][:, u * P : (u + 1) * P], vcols[:, r : r + 1].to_broadcast([P, P]), ident[:]
                )

        def keep_bias(q):
            words = min(4, UNITS - 4 * q) * P
            cols = slice(q * PIECE, q * PIECE + 2 * words)
            nc.scalar.copy(out=bias_sb[:, cols].bitcast(F32), in_=spread[q][:, 0:words])

        def unit_rows(i):
            return weight[i * UNIT : (i + 1) * UNIT, :].rearrange("(p j) k -> p j k", j=2)

        def load_unit(i):
            if i not in TURNED:
                for a in range(parts(i)):
                    load_part(i, a)

        def load_turned(i, h):
            if i not in raw:
                raw[i] = rawt_pool.tile([P, 4 * CHUNK, P], BF16, name="raw%d" % i, tag="rawt")
            src = weight.rearrange("n k -> (n k)")[i * UNIT * K : (i + 1) * UNIT * K].rearrange(
                "(b r s k) -> b r s k", r=4 * CHUNK, s=4, k=P
            )
            rows = slice(2 * CHUNK * h, 2 * CHUNK * (h + 1))
            for q in range(4):
                nc.sync.dma_start(out=raw[i][32 * q : 32 * q + 32, rows, :], in_=src[:, rows, q, :])

        def load_ws_turned():
            src = ws_vec.rearrange("(i b c) -> b i c", b=32, c=CHUNK)[:, TURNED[0] : TURNED[-1] + 1 : TURNED[1] - TURNED[0], :]
            for q in range(4):
                nc.sync.dma_start(out=ws_turn[32 * q : 32 * q + 32, :, 0:CHUNK], in_=src)

        chunk = {}
        turned = {}

        def prescale_turned(i, c):
            w = 2 * K // CHUNK
            chunk[(i, c)] = sclt_pool.tile([P, w], BF16, name="sclt%d_%d" % (i, c), tag="sclt", align_bytes=64)
            nc.scalar.activation(
                out=chunk[(i, c)][:].rearrange("p (u w e) -> p u w e", u=2, e=16),
                in_=raw[i][:].rearrange("p r k -> p (r k)")[:, c * w : (c + 1) * w].rearrange("p (w u e) -> p u w e", u=2, e=16),
                func=COPY,
                scale=ws_turn_f32[:, TURNED.index(i), c : c + 1],
            )

        def turn(i, c):
            if i not in turned:
                turned[i] = turn_pool.tile([P, K], F32, name="turn%d" % i, tag="turn", align_bytes=64)
            w = K // CHUNK
            nc.vector.transpose(out=turned[i][:, c * w : (c + 1) * w], in_=chunk[(i, c)][:].bitcast(F32))

        def interleave(i):
            grp[i] = grp_pool.tile([P, PASSES * 4 * UNIT], BF16, name="grp%d" % i, tag="grp", align_bytes=64)
            for g in range(PASSES):
                nc.scalar.copy(
                    out=grp[i][:, g * 1024 : (g + 1) * 1024].bitcast(F32).rearrange("p (c b u) -> p c b u", c=CHUNK, u=2),
                    in_=turned[i][:].rearrange("p (c u g b) -> p g c b u", c=CHUNK, u=2, g=4)[:, g, :, :, :],
                )

        def parts(i):
            return 2 if i == 0 else 1

        def load_part(i, a):
            n = parts(i)
            w = K // n
            if i not in raw:
                raw[i] = raw_pool.tile([P, n, 2, w], BF16, name="raw%d" % i, tag="raw")
            nc.sync.dma_start(out=raw[i][:, a, :, :], in_=unit_rows(i)[:, :, a * w : (a + 1) * w])

        def prescale(i, a):
            n = parts(i)
            if i not in scl:
                scl[i] = scl_pool.tile([P, n, 2, K // n], BF16, name="scl%d" % i, tag="scl", align_bytes=64)
            for j in range(2):
                c = 2 * vector_row(i) + j
                nc.vector.tensor_scalar(
                    out=scl[i][:, a, j, :].rearrange("p (u w e) -> p u w e", u=2, e=16),
                    in0=raw[i][:, a, j, :].rearrange("p (w u e) -> p u w e", u=2, e=16),
                    scalar1=ws_cols[:, c : c + 1],
                    scalar2=None,
                    op0=MULT,
                )

        def prescale_unit(i):
            for a in range(parts(i)):
                prescale(i, a)

        wbank = {}

        def transpose_pass(i, g, copy):
            if i not in grp:
                grp[i] = grp_pool.tile([P, PASSES * 4 * UNIT], BF16, name="grp%d" % i, tag="grp", align_bytes=64)
            bank = tp_pool.tile([P, 512], F32, name="tp%d_%d" % (i, g), tag="tp")
            per = PASSES // parts(i)
            for j in range(2):
                words = scl[i][:, g // per, j, :].bitcast(F32)
                for h in range(2):
                    s = 2 * j + h
                    blk = per * h + g % per
                    nc.tensor.transpose(
                        bank[:, s * P : (s + 1) * P], words[:, blk * P : (blk + 1) * P], ident[:]
                    )
            wbank[(i, g)] = bank
            if copy is not None:
                copy_pass(i, g, copy)

        def copy_pass(i, g, copy):
            copy(
                out=grp[i][:, g * 1024 : (g + 1) * 1024].bitcast(F32).rearrange("p (c s) -> p c s", s=4),
                in_=wbank[(i, g)][:].rearrange("p (s c) -> p c s", s=4),
            )

        def transpose_unit(i):
            for g in range(PASSES):
                transpose_pass(i, g, nc.scalar.copy)

        def quantise(i, g0, g1):
            if i not in codes:
                codes[i] = code_pool.tile([P, PASSES * UNIT], U32, name="codes%d" % i, tag="codes", align_bytes=64)
                plane[i] = code_pool.tile([P, PASSES * UNIT], U8, name="plane%d" % i, tag="plane", align_bytes=64)
            cols = slice(g0 * UNIT, g1 * UNIT)
            nc.vector.quantize_mx(
                out=codes[i][:, cols].bitcast(FP8X4),
                scales=plane[i][:, cols],
                in_=grp[i][:, 4 * g0 * UNIT : 4 * g1 * UNIT],
            )

        def multiply(i, m):
            b = m // 2
            if (i, b) not in acc:
                acc[(i, b)] = acc_pool.tile([P, 512], F32, name="acc%d_%d" % (i, b), tag="acc")
            for g in range(PASSES):
                nc.tensor.matmul_mx(
                    out=acc[(i, b)][:, (m % 2) * UNIT : (m % 2 + 1) * UNIT],
                    lhsT=xcodes[:, m, g * P : (g + 1) * P].bitcast(FP8X4),
                    lhsT_scale=xplane[:, m, g * P : (g + 1) * P],
                    rhs=codes[i][:, g * UNIT : (g + 1) * UNIT].bitcast(FP8X4),
                    rhs_scale=plane[i][:, g * UNIT : (g + 1) * UNIT],
                    start=(g == 0),
                    stop=(g == PASSES - 1),
                )

        def finish(i, b):
            gi = group_of[i]
            if gi not in stage:
                stage[gi] = stage_pool.tile([P, MT, 2 * UNIT], F32, name="stage%d" % gi, tag="stage")
            off = (i - group_start[gi]) * UNIT
            row = bias_sb[:, i * UNIT : (i + 1) * UNIT].unsqueeze(1).to_broadcast([P, 2, UNIT])
            result = stage[gi][:, 2 * b : 2 * b + 2, off : off + UNIT]
            product = acc[(i, b)][:].rearrange("p (m n) -> p m n", m=2)
            if i in TURNED:
                row = row.rearrange("p m (b c) -> p m b c", c=CHUNK)
                result = result.rearrange("p m (b c) -> p m b c", c=CHUNK)
                product = acc[(i, b)][:].rearrange("p (m c b) -> p m b c", m=2, c=CHUNK)
            nc.vector.tensor_tensor(out=result, in0=product, in1=row, op=ADD)
            if b == 1 and i == group_start[gi] + GROUP_SIZES[gi] - 1:
                a = group_start[gi] * UNIT
                w = GROUP_SIZES[gi] * UNIT
                nc.sync.dma_start(out=out_rows[:, :, a : a + w], in_=stage[gi][:, :, 0:w])

        xdei = {}

        def split_x(m):
            xdei[m] = xdei_pool.tile([P, K], BF16, name="xdei%d" % m, tag="xdei")
            nc.vector.tensor_copy(
                out=xdei[m][:].rearrange("p (u w e) -> p u w e", u=2, e=16),
                in_=xraw[:, m, :].rearrange("p (w u e) -> p u w e", u=2, e=16),
            )

        def finish_last(m):
            i = UNITS - 1
            gi = group_of[i]
            if gi not in stage:
                stage[gi] = stage_pool.tile([P, MT, 2 * UNIT], F32, name="stage%d" % gi, tag="stage")
            nc.vector.tensor_tensor(
                out=stage[gi][:, m, 0:UNIT],
                in0=acc[(i, m // 2)][:, (m % 2) * UNIT : (m % 2 + 1) * UNIT],
                in1=bias_sb[:, i * UNIT : (i + 1) * UNIT],
                op=ADD,
            )
            nc.sync.dma_start(out=out_rows[:, m, i * UNIT : (i + 1) * UNIT], in_=stage[gi][:, m, 0:UNIT])

        xbank = {}

        def transpose_x(m, b):
            xbank[(m, b)] = tp_pool.tile([P, 512], F32, name="tpx%d_%d" % (m, b), tag="tp")
            words = xdei[m][:].bitcast(F32)
            for s in range(4):
                blk = PASSES * (s % 2) + 2 * b + s // 2
                nc.tensor.transpose(
                    xbank[(m, b)][:, s * P : (s + 1) * P], words[:, blk * P : (blk + 1) * P], ident[:]
                )

        def copy_x(m, b, copy):
            if m not in xg:
                xg[m] = xg_pool.tile([P, PASSES * 4 * P], BF16, name="xg%d" % m, tag="xg", align_bytes=64)
            copy(
                out=xg[m][:, b * 1024 : (b + 1) * 1024].bitcast(F32).rearrange("p (g c h) -> p g c h", g=2, h=2),
                in_=xbank[(m, b)][:].rearrange("p (g h c) -> p g c h", g=2, h=2),
            )

        def quantise_x(m):
            nc.vector.quantize_mx(out=xcodes[:, m, :].bitcast(FP8X4), scales=xplane[:, m, :], in_=xg[m][:])

        nc.sync.dma_start(out=xraw[:, 0, :], in_=x_rows[:, 0, :])
        nc.vector.memset(vrows[:].bitcast(I32), 0)
        nc.vector.memset(zeros[:].bitcast(I32), 0)
        nc.scalar.copy(out=scratch[:, 1:2], in_=zeros[:, 0:1])
        make_identity(nc, ident[:])
        for row, vec in ((0, ws_vec), (BIAS_ROW, bias_vec)):
            rows = vec.rearrange("(r n) -> r n", n=UNIT)
            nc.sync.dma_start(out=vrows[row : row + FIRST_ROWS, :], in_=rows[0:FIRST_ROWS, :])
            rest = row + FIRST_ROWS
            nc.sync.dma_start(out=vrows[rest : rest + REST_ROWS, :], in_=rows[UNITS - REST_ROWS : UNITS, :])
        load_unit(0)
        for m in range(1, MT):
            nc.sync.dma_start(out=xraw[:, m, :], in_=x_rows[:, m, :])
        for i in range(1, RAW_BUFS):
            load_unit(i)

        warm_bank = acc_pool.tile([P, 512], F32, name="warm", tag="acc")
        warm_up(warm_bank, 4)
        col_bank = acc_pool.tile([P, 512], F32, name="col_bank", tag="acc")
        nc.tensor.transpose(col_bank[:, 0:P], vrows[:].bitcast(F32), ident[:])
        split_x(0)
        nc.vector.tensor_copy(out=vcols[:], in_=col_bank[:, 0:P])
        transpose_x(0, 0)
        copy_x(0, 0, nc.scalar.copy)
        transpose_x(0, 1)
        prescale(0, 0)
        copy_x(0, 1, nc.vector.tensor_copy)
        transpose_pass(0, 0, nc.scalar.copy)
        transpose_pass(0, 1, nc.scalar.copy)
        prescale(0, 1)
        quantise_x(0)
        split_x(1)
        transpose_pass(0, 2, nc.scalar.copy)
        transpose_pass(0, 3, nc.scalar.copy)
        spread_bias(0, acc_pool, "acc")
        spread_bias(1, acc_pool, "acc")
        quantise(0, 0, 2)
        transpose_x(1, 0)
        copy_x(1, 0, nc.scalar.copy)
        transpose_x(1, 1)
        copy_x(1, 1, nc.scalar.copy)
        split_x(2)
        transpose_x(2, 0)
        copy_x(2, 0, nc.scalar.copy)
        transpose_x(2, 1)
        copy_x(2, 1, nc.scalar.copy)
        quantise(0, 2, 4)
        multiply(0, 0)
        split_x(3)
        quantise_x(1)
        transpose_x(3, 0)
        copy_x(3, 0, nc.scalar.copy)
        transpose_x(3, 1)
        copy_x(3, 1, nc.scalar.copy)
        multiply(0, 1)
        keep_bias(0)
        quantise_x(2)
        prescale_unit(1)
        multiply(0, 2)
        transpose_unit(1)
        keep_bias(1)
        quantise_x(3)
        multiply(0, 3)
        prescale_unit(2)
        quantise(1, 0, 2)
        quantise(1, 2, 4)
        transpose_unit(2)
        finish(0, 0)
        finish(0, 1)
        prescale_unit(3)

        loads = RAW_BUFS
        lead = TURNED[0]
        begin = {}
        for v in TURNED:
            begin[v] = v - 7

        def run_unit(i):
            return i + 2 if i + 2 < lead else i + 3

        def chunks_of(v, i):
            span = v - 3 - begin[v]
            return [c for c in range(CHUNK) if begin[v] + c * span // CHUNK == i]

        for i in range(1, UNITS):
            for m in range(MT):
                multiply(i, m)
                if m == 1 and 2 * i < PIECES:
                    for q in (2 * i, 2 * i + 1):
                        spread_bias(q, tp_pool, "tp")
                        keep_bias(q)
            if i == 1:
                load_ws_turned()
            for v in TURNED:
                for h in range(2):
                    if i == max(1, begin[v] - 4 + 1 * h):
                        load_turned(v, h)
            while loads < UNITS and loads <= i + 10:
                if loads not in TURNED:
                    load_unit(loads)
                loads += 1
            if run_unit(i - 1) < UNITS - 1:
                quantise(run_unit(i - 1), 0, 4)
            elif run_unit(i - 1) < UNITS:
                quantise(run_unit(i - 1), 0, 2)
                quantise(run_unit(i - 1), 2, 4)
            if i == lead - 2:
                quantise(lead, 0, 4)
            if i == begin[TURNED[0]] - 1:
                for v in range(len(TURNED)):
                    nc.vector.tensor_copy(out=ws_turn_f32[:, v, :], in_=ws_turn[:, v, 0:CHUNK])
            for v in TURNED:
                for c in chunks_of(v, i - 1):
                    turn(v, c)
            if run_unit(i) < UNITS and run_unit(i) not in TURNED:
                transpose_unit(run_unit(i))
            for v in TURNED:
                if i == v - 3:
                    interleave(v)
                for c in chunks_of(v, i):
                    prescale_turned(v, c)
            if run_unit(i + 1) < UNITS and run_unit(i + 1) not in TURNED:
                prescale_unit(run_unit(i + 1))
            if i < UNITS - 1:
                finish(i, 0)
                finish(i, 1)
            else:
                for m in range(MT):
                    finish_last(m)
